import numpy as np
import ml_dtypes

BF16 = ml_dtypes.bfloat16


def bf(x):
    return np.asarray(x, np.float32).astype(BF16)


def f32(x):
    return np.asarray(x, np.float32)


def f64(x):
    return np.asarray(x).astype(np.float64)


def striped(idx):
    return np.tile(idx.reshape(-1, 16).T, (8, 1))


C, S, R, T, NS, N = 512, 4096, 4, 512, 32, 2048


def setup_inputs():
    return {
        "table": f32(np.random.standard_normal((C, S))),
        "days": f32(2.0 * np.random.random((1, N))),
        "value": f32(np.random.standard_normal((1, N))),
        "has_value": f32(np.random.random((1, N)) < 0.5),
        "date_w": f32(np.random.standard_normal((C, 1))),
        "date_b": f32(0.1 * np.random.standard_normal((C, 1))),
        "val_w": f32(np.random.standard_normal((C, 1))),
        "val_b": f32(0.1 * np.random.standard_normal((C, 1))),
        "offs": striped(np.random.permutation(np.tile(np.arange(S), 2))[:N]),
    }


def reference(table, days, value, has_value, date_w, date_b, val_w, val_b, offs):
    idx = offs[:16].T.reshape(-1)
    dyn = np.tile((np.arange(T) >= NS).astype(np.float64), R)[None, :]
    time_emb = (f64(days) * f64(date_w) + f64(date_b)) * dyn
    val_emb = (f64(value) * f64(val_w) + f64(val_b)) * f64(has_value)
    emb = f64(table)[:, idx] + time_emb + val_emb
    e3 = emb.reshape(C, R, T)
    res = e3.copy()
    res[:, :, NS] = e3[:, :, NS:].sum(axis=2) / (T - NS)
    return res.reshape(C, N)

@@ -1,0 +1,104 @@
+import concourse.mybir as mybir
+
+F32 = mybir.dt.float32
+U16 = mybir.dt.uint16
+ADD = mybir.AluOpType.add
+MULT = mybir.AluOpType.mult
+COPY = mybir.ActivationFunctionType.Copy
+
+P = 128
+CHANNELS, CODES = 512, 4096
+RECORDS, TOKENS, STATIC = 4, 512, 32
+DYNAMIC = TOKENS - STATIC
+N = RECORDS * TOKENS
+BLOCKS = CHANNELS // P
+LIST_COLUMNS = TOKENS // 16
+PIECES = BLOCKS * RECORDS
+AHEAD = 4
+
+ROW_VALUE = 0
+ROW_HAS = 32
+ROW_DAYS = 64
+ROW_DYN = 96
+
+FLOPS = 2 * 4 * CHANNELS * N
+
+
+def tile_hybridsummaryencoder_kernel(
+    tc, table, days, value, has_value, date_w, date_b, val_w, val_b, offs, out
+):
+    nc = tc.nc
+    with (
+        tc.tile_pool(name="held", bufs=1) as held,
+        tc.tile_pool(name="ahead", bufs=AHEAD + 2) as ahead,
+        tc.tile_pool(name="scratch", bufs=2) as scratch,
+        tc.psum_pool(name="psum", bufs=4) as psum,
+    ):
+        offsets = held.tile([P, N // 16], U16, name="offsets")
+        nc.sync.dma_start(offsets[:], offs)
+        tables = []
+        for b in range(BLOCKS):
+            block = held.tile([P, CODES], F32, name=f"table{b}")
+            nc.sync.dma_start(block[:], table[b * P : (b + 1) * P, :])
+            tables.append(block)
+
+        value_row = held.tile([1, N], F32, name="value_row")
+        has_row = held.tile([1, N], F32, name="has_row")
+        nc.scalar.dma_start(value_row[:], value)
+        nc.scalar.dma_start(has_row[:], has_value)
+
+        coefs = held.tile([P, CHANNELS], F32, name="coefs")
+        nc.vector.memset(coefs[:], 0.0)
+        for row, vector in ((ROW_VALUE, val_w), (ROW_HAS, val_b), (ROW_DAYS, date_w), (ROW_DYN, date_b)):
+            nc.scalar.dma_start(coefs[row : row + 1, :], vector.rearrange("c o -> o c"))
+
+        features = held.tile([P, N], F32, name="features")
+        by_record = features[:].rearrange("k (r t) -> k r t", t=TOKENS)
+        nc.vector.memset(by_record[:, :, STATIC:], 1.0)
+        nc.vector.memset(by_record[:, :, :STATIC], 0.0)
+        nc.scalar.dma_start(features[ROW_HAS : ROW_HAS + 1, :], has_value)
+        nc.scalar.dma_start(
+            by_record[ROW_DAYS : ROW_DAYS + 1, :, STATIC:],
+            days.rearrange("o (r t) -> o r t", t=TOKENS)[:, :, STATIC:],
+        )
+
+        for r in range(RECORDS):
+            tokens = slice(r * TOKENS, (r + 1) * TOKENS)
+            nc.vector.tensor_tensor(
+                features[ROW_VALUE : ROW_VALUE + 1, tokens], value_row[:, tokens], has_row[:, tokens], MULT
+            )
+
+        embs = [held.tile([P, N], F32, name=f"emb{b}") for b in range(BLOCKS)]
+        terms_of = {}
+
+        for step in range(PIECES + AHEAD):
+            if step < PIECES:
+                b, r = divmod(step, RECORDS)
+                product = psum.tile([P, TOKENS], F32, name="product")
+                nc.tensor.matmul(
+                    product[:],
+                    coefs[:, b * P : (b + 1) * P],
+                    features[:, r * TOKENS : (r + 1) * TOKENS],
+                    start=True,
+                    stop=True,
+                )
+                terms = ahead.tile([P, TOKENS], F32, name="terms")
+                nc.scalar.copy(terms[:], product[:])
+                terms_of[step] = terms
+
+            if step >= AHEAD:
+                b, r = divmod(step - AHEAD, RECORDS)
+                emb = embs[b]
+                tokens = slice(r * TOKENS, (r + 1) * TOKENS)
+                dynamic = slice(r * TOKENS + STATIC, (r + 1) * TOKENS)
+                summary = slice(r * TOKENS + STATIC, r * TOKENS + STATIC + 1)
+
+                picked = tables[b][:].indirect(offsets[:, r * LIST_COLUMNS : (r + 1) * LIST_COLUMNS])
+                nc.vector.tensor_tensor(emb[:, tokens], picked, terms_of[step - AHEAD][:], ADD)
+
+                scaled = scratch.tile([P, DYNAMIC], F32, name="scaled")
+                mean = scratch.tile([P, 1], F32, name="mean")
+                nc.scalar.activation(scaled[:], emb[:, dynamic], COPY, scale=1.0 / DYNAMIC, accum_out=mean[:])
+                nc.scalar.copy(emb[:, summary], mean[:])
+
+                nc.sync.dma_start(out[b * P : (b + 1) * P, tokens], emb[:, tokens])

@@ -34,28 +34,27 @@ def tile_hybridsummaryencoder_kernel(
         tc.tile_pool(name="scratch", bufs=2) as scratch,
         tc.psum_pool(name="psum", bufs=4) as psum,
     ):
+        tables = [held.tile([P, CODES], F32, name=f"table{b}") for b in range(BLOCKS)]
+        embs = [held.tile([P, N], F32, name=f"emb{b}") for b in range(BLOCKS)]
         offsets = held.tile([P, N // 16], U16, name="offsets")
-        nc.sync.dma_start(offsets[:], offs)
-        tables = []
-        for b in range(BLOCKS):
-            block = held.tile([P, CODES], F32, name=f"table{b}")
-            nc.sync.dma_start(block[:], table[b * P : (b + 1) * P, :])
-            tables.append(block)
-
+        coefs = held.tile([P, CHANNELS], F32, name="coefs")
+        features = held.tile([P, N], F32, name="features")
         value_row = held.tile([1, N], F32, name="value_row")
         has_row = held.tile([1, N], F32, name="has_row")
-        nc.scalar.dma_start(value_row[:], value)
-        nc.scalar.dma_start(has_row[:], has_value)
-
-        coefs = held.tile([P, CHANNELS], F32, name="coefs")
-        nc.vector.memset(coefs[:], 0.0)
-        for row, vector in ((ROW_VALUE, val_w), (ROW_HAS, val_b), (ROW_DAYS, date_w), (ROW_DYN, date_b)):
-            nc.scalar.dma_start(coefs[row : row + 1, :], vector.rearrange("c o -> o c"))
-
-        features = held.tile([P, N], F32, name="features")
         by_record = features[:].rearrange("k (r t) -> k r t", t=TOKENS)
+
+        nc.vector.memset(coefs[:], 0.0)
         nc.vector.memset(by_record[:, :, STATIC:], 1.0)
         nc.vector.memset(by_record[:, :, :STATIC], 0.0)
+
+        nc.sync.dma_start(tables[0][:], table[0:P, :])
+        nc.sync.dma_start(offsets[:], offs)
+        for b in range(1, BLOCKS):
+            nc.sync.dma_start(tables[b][:], table[b * P : (b + 1) * P, :])
+        nc.scalar.dma_start(value_row[:], value)
+        nc.scalar.dma_start(has_row[:], has_value)
+        for row, vector in ((ROW_VALUE, val_w), (ROW_HAS, val_b), (ROW_DAYS, date_w), (ROW_DYN, date_b)):
+            nc.scalar.dma_start(coefs[row : row + 1, :], vector.rearrange("c o -> o c"))
         nc.scalar.dma_start(features[ROW_HAS : ROW_HAS + 1, :], has_value)
         nc.scalar.dma_start(
             by_record[ROW_DAYS : ROW_DAYS + 1, :, STATIC:],
@@ -68,7 +67,6 @@ def tile_hybridsummaryencoder_kernel(
                 features[ROW_VALUE : ROW_VALUE + 1, tokens], value_row[:, tokens], has_row[:, tokens], MULT
             )
 
-        embs = [held.tile([P, N], F32, name=f"emb{b}") for b in range(BLOCKS)]
         terms_of = {}
 
         for step in range(PIECES + AHEAD):
@@ -89,6 +87,7 @@ def tile_hybridsummaryencoder_kernel(
             if step >= AHEAD:
                 b, r = divmod(step - AHEAD, RECORDS)
                 emb = embs[b]
+                channels = slice(b * P, (b + 1) * P)
                 tokens = slice(r * TOKENS, (r + 1) * TOKENS)
                 dynamic = slice(r * TOKENS + STATIC, (r + 1) * TOKENS)
                 summary = slice(r * TOKENS + STATIC, r * TOKENS + STATIC + 1)
@@ -97,8 +96,11 @@ def tile_hybridsummaryencoder_kernel(
                 nc.vector.tensor_tensor(emb[:, tokens], picked, terms_of[step - AHEAD][:], ADD)
 
                 scaled = scratch.tile([P, DYNAMIC], F32, name="scaled")
-                mean = scratch.tile([P, 1], F32, name="mean")
-                nc.scalar.activation(scaled[:], emb[:, dynamic], COPY, scale=1.0 / DYNAMIC, accum_out=mean[:])
-                nc.scalar.copy(emb[:, summary], mean[:])
+                nc.scalar.activation(
+                    scaled[:], emb[:, dynamic], COPY, scale=1.0 / DYNAMIC, accum_out=emb[:, summary]
+                )
 
-                nc.sync.dma_start(out[b * P : (b + 1) * P, tokens], emb[:, tokens])
+                if b == BLOCKS - 1:
+                    nc.sync.dma_start(out[channels, tokens], emb[:, tokens])
+                elif r == RECORDS - 1:
+                    nc.sync.dma_start(out[channels, :], emb[:])

@@ -15,6 +15,7 @@ BLOCKS = CHANNELS // P
 LIST_COLUMNS = TOKENS // 16
 PIECES = BLOCKS * RECORDS
 AHEAD = 4
+WARMUP = 10
 
 ROW_VALUE = 0
 ROW_HAS = 32
@@ -33,6 +34,7 @@ def tile_hybridsummaryencoder_kernel(
         tc.tile_pool(name="ahead", bufs=AHEAD + 2) as ahead,
         tc.tile_pool(name="scratch", bufs=2) as scratch,
         tc.psum_pool(name="psum", bufs=4) as psum,
+        tc.psum_pool(name="spare", bufs=1) as spare,
     ):
         tables = [held.tile([P, CODES], F32, name=f"table{b}") for b in range(BLOCKS)]
         embs = [held.tile([P, N], F32, name=f"emb{b}") for b in range(BLOCKS)]
@@ -41,15 +43,17 @@ def tile_hybridsummaryencoder_kernel(
         features = held.tile([P, N], F32, name="features")
         value_row = held.tile([1, N], F32, name="value_row")
         has_row = held.tile([1, N], F32, name="has_row")
+        zeros = held.tile([P, P], F32, name="zeros")
         by_record = features[:].rearrange("k (r t) -> k r t", t=TOKENS)
 
-        nc.vector.memset(coefs[:], 0.0)
-        nc.vector.memset(by_record[:, :, STATIC:], 1.0)
-        nc.vector.memset(by_record[:, :, :STATIC], 0.0)
+        nc.gpsimd.memset(zeros[:], 0.0)
+        nc.gpsimd.memset(coefs[:], 0.0)
+        for engine, records in ((nc.vector, slice(0, RECORDS - 1)), (nc.gpsimd, slice(RECORDS - 1, RECORDS))):
+            engine.memset(by_record[:, records, STATIC:], 1.0)
+            engine.memset(by_record[:, records, :STATIC], 0.0)
 
-        nc.sync.dma_start(tables[0][:], table[0:P, :])
         nc.sync.dma_start(offsets[:], offs)
-        for b in range(1, BLOCKS):
+        for b in range(BLOCKS):
             nc.sync.dma_start(tables[b][:], table[b * P : (b + 1) * P, :])
         nc.scalar.dma_start(value_row[:], value)
         nc.scalar.dma_start(has_row[:], has_value)
@@ -60,6 +64,10 @@ def tile_hybridsummaryencoder_kernel(
             by_record[ROW_DAYS : ROW_DAYS + 1, :, STATIC:],
             days.rearrange("o (r t) -> o r t", t=TOKENS)[:, :, STATIC:],
         )
+
+        unused = spare.tile([P, P], F32, name="unused")
+        for w in range(WARMUP):
+            nc.tensor.matmul(unused[:], zeros[:], zeros[:], start=True, stop=True)
 
         for r in range(RECORDS):
             tokens = slice(r * TOKENS, (r + 1) * TOKENS)

@@ -52,18 +52,18 @@ def tile_hybridsummaryencoder_kernel(
             engine.memset(by_record[:, records, STATIC:], 1.0)
             engine.memset(by_record[:, records, :STATIC], 0.0)
 
-        nc.sync.dma_start(offsets[:], offs)
-        for b in range(BLOCKS):
-            nc.sync.dma_start(tables[b][:], table[b * P : (b + 1) * P, :])
-        nc.scalar.dma_start(value_row[:], value)
-        nc.scalar.dma_start(has_row[:], has_value)
+        nc.sync.dma_start(value_row[:], value)
+        nc.sync.dma_start(has_row[:], has_value)
         for row, vector in ((ROW_VALUE, val_w), (ROW_HAS, val_b), (ROW_DAYS, date_w), (ROW_DYN, date_b)):
-            nc.scalar.dma_start(coefs[row : row + 1, :], vector.rearrange("c o -> o c"))
-        nc.scalar.dma_start(features[ROW_HAS : ROW_HAS + 1, :], has_value)
-        nc.scalar.dma_start(
+            nc.sync.dma_start(coefs[row : row + 1, :], vector.rearrange("c o -> o c"))
+        nc.sync.dma_start(features[ROW_HAS : ROW_HAS + 1, :], has_value)
+        nc.sync.dma_start(
             by_record[ROW_DAYS : ROW_DAYS + 1, :, STATIC:],
             days.rearrange("o (r t) -> o r t", t=TOKENS)[:, :, STATIC:],
         )
+        nc.sync.dma_start(offsets[:], offs)
+        for b in range(BLOCKS):
+            nc.sync.dma_start(tables[b][:], table[b * P : (b + 1) * P, :])
 
         unused = spare.tile([P, P], F32, name="unused")
         for w in range(WARMUP):

@@ -18,9 +18,10 @@ AHEAD = 4
 WARMUP = 10
 
 ROW_VALUE = 0
-ROW_HAS = 32
-ROW_DAYS = 64
-ROW_DYN = 96
+ROW_DYN = 1
+ROW_HAS = 126
+ROW_DAYS = 127
+FILLED = 126
 
 FLOPS = 2 * 4 * CHANNELS * N
 
@@ -46,21 +47,21 @@ def tile_hybridsummaryencoder_kernel(
         zeros = held.tile([P, P], F32, name="zeros")
         by_record = features[:].rearrange("k (r t) -> k r t", t=TOKENS)
 
+        nc.vector.memset(by_record[:, :, :STATIC], 0.0)
+        nc.gpsimd.memset(coefs[:FILLED, :], 0.0)
         nc.gpsimd.memset(zeros[:], 0.0)
-        nc.gpsimd.memset(coefs[:], 0.0)
-        for engine, records in ((nc.vector, slice(0, RECORDS - 1)), (nc.gpsimd, slice(RECORDS - 1, RECORDS))):
-            engine.memset(by_record[:, records, STATIC:], 1.0)
-            engine.memset(by_record[:, records, :STATIC], 0.0)
+        nc.vector.memset(by_record[:FILLED, : RECORDS - 1, STATIC:], 1.0)
+        nc.gpsimd.memset(by_record[:FILLED, RECORDS - 1 :, STATIC:], 1.0)
 
         nc.sync.dma_start(value_row[:], value)
         nc.sync.dma_start(has_row[:], has_value)
-        for row, vector in ((ROW_VALUE, val_w), (ROW_HAS, val_b), (ROW_DAYS, date_w), (ROW_DYN, date_b)):
-            nc.sync.dma_start(coefs[row : row + 1, :], vector.rearrange("c o -> o c"))
-        nc.sync.dma_start(features[ROW_HAS : ROW_HAS + 1, :], has_value)
         nc.sync.dma_start(
             by_record[ROW_DAYS : ROW_DAYS + 1, :, STATIC:],
             days.rearrange("o (r t) -> o r t", t=TOKENS)[:, :, STATIC:],
         )
+        for row, vector in ((ROW_HAS, val_b), (ROW_DAYS, date_w), (ROW_VALUE, val_w), (ROW_DYN, date_b)):
+            nc.sync.dma_start(coefs[row : row + 1, :], vector.rearrange("c o -> o c"))
+        nc.sync.dma_start(features[ROW_HAS : ROW_HAS + 1, :], has_value)
         nc.sync.dma_start(offsets[:], offs)
         for b in range(BLOCKS):
             nc.sync.dma_start(tables[b][:], table[b * P : (b + 1) * P, :])

@@ -15,7 +15,6 @@ BLOCKS = CHANNELS // P
 LIST_COLUMNS = TOKENS // 16
 PIECES = BLOCKS * RECORDS
 AHEAD = 4
-WARMUP = 10
 
 ROW_VALUE = 0
 ROW_DYN = 1
@@ -35,7 +34,6 @@ def tile_hybridsummaryencoder_kernel(
         tc.tile_pool(name="ahead", bufs=AHEAD + 2) as ahead,
         tc.tile_pool(name="scratch", bufs=2) as scratch,
         tc.psum_pool(name="psum", bufs=4) as psum,
-        tc.psum_pool(name="spare", bufs=1) as spare,
     ):
         tables = [held.tile([P, CODES], F32, name=f"table{b}") for b in range(BLOCKS)]
         embs = [held.tile([P, N], F32, name=f"emb{b}") for b in range(BLOCKS)]
@@ -44,12 +42,10 @@ def tile_hybridsummaryencoder_kernel(
         features = held.tile([P, N], F32, name="features")
         value_row = held.tile([1, N], F32, name="value_row")
         has_row = held.tile([1, N], F32, name="has_row")
-        zeros = held.tile([P, P], F32, name="zeros")
         by_record = features[:].rearrange("k (r t) -> k r t", t=TOKENS)
 
         nc.vector.memset(by_record[:, :, :STATIC], 0.0)
         nc.gpsimd.memset(coefs[:FILLED, :], 0.0)
-        nc.gpsimd.memset(zeros[:], 0.0)
         nc.vector.memset(by_record[:FILLED, : RECORDS - 1, STATIC:], 1.0)
         nc.gpsimd.memset(by_record[:FILLED, RECORDS - 1 :, STATIC:], 1.0)
 
@@ -65,10 +61,6 @@ def tile_hybridsummaryencoder_kernel(
         nc.sync.dma_start(offsets[:], offs)
         for b in range(BLOCKS):
             nc.sync.dma_start(tables[b][:], table[b * P : (b + 1) * P, :])
-
-        unused = spare.tile([P, P], F32, name="unused")
-        for w in range(WARMUP):
-            nc.tensor.matmul(unused[:], zeros[:], zeros[:], start=True, stop=True)
 
         for r in range(RECORDS):
             tokens = slice(r * TOKENS, (r + 1) * TOKENS)

@@ -45,9 +45,8 @@ def tile_hybridsummaryencoder_kernel(
         by_record = features[:].rearrange("k (r t) -> k r t", t=TOKENS)
 
         nc.vector.memset(by_record[:, :, :STATIC], 0.0)
-        nc.gpsimd.memset(coefs[:FILLED, :], 0.0)
-        nc.vector.memset(by_record[:FILLED, : RECORDS - 1, STATIC:], 1.0)
-        nc.gpsimd.memset(by_record[:FILLED, RECORDS - 1 :, STATIC:], 1.0)
+        nc.vector.memset(coefs[:FILLED, :], 0.0)
+        nc.vector.memset(by_record[:FILLED, :, STATIC:], 1.0)
 
         nc.sync.dma_start(value_row[:], value)
         nc.sync.dma_start(has_row[:], has_value)

@@ -5,6 +5,7 @@ U16 = mybir.dt.uint16
 ADD = mybir.AluOpType.add
 MULT = mybir.AluOpType.mult
 COPY = mybir.ActivationFunctionType.Copy
+IDENTITY = mybir.ActivationFunctionType.Identity
 
 P = 128
 CHANNELS, CODES = 512, 4096
@@ -15,6 +16,7 @@ BLOCKS = CHANNELS // P
 LIST_COLUMNS = TOKENS // 16
 PIECES = BLOCKS * RECORDS
 AHEAD = 4
+HEAD = 128
 
 ROW_VALUE = 0
 ROW_DYN = 1
@@ -87,20 +89,54 @@ def tile_hybridsummaryencoder_kernel(
             if step >= AHEAD:
                 b, r = divmod(step - AHEAD, RECORDS)
                 emb = embs[b]
+                terms = terms_of[step - AHEAD]
                 channels = slice(b * P, (b + 1) * P)
-                tokens = slice(r * TOKENS, (r + 1) * TOKENS)
-                dynamic = slice(r * TOKENS + STATIC, (r + 1) * TOKENS)
-                summary = slice(r * TOKENS + STATIC, r * TOKENS + STATIC + 1)
+                start = r * TOKENS
+                summary = slice(start + STATIC, start + STATIC + 1)
 
-                picked = tables[b][:].indirect(offsets[:, r * LIST_COLUMNS : (r + 1) * LIST_COLUMNS])
-                nc.vector.tensor_tensor(emb[:, tokens], picked, terms_of[step - AHEAD][:], ADD)
+                if step - AHEAD < PIECES - 1:
+                    picked = tables[b][:].indirect(offsets[:, r * LIST_COLUMNS : (r + 1) * LIST_COLUMNS])
+                    nc.vector.tensor_tensor(emb[:, start : start + TOKENS], picked, terms[:], ADD)
 
-                scaled = scratch.tile([P, DYNAMIC], F32, name="scaled")
-                nc.scalar.activation(
-                    scaled[:], emb[:, dynamic], COPY, scale=1.0 / DYNAMIC, accum_out=emb[:, summary]
-                )
+                    scaled = scratch.tile([P, DYNAMIC], F32, name="scaled")
+                    nc.scalar.activation(
+                        scaled[:],
+                        emb[:, start + STATIC : start + TOKENS],
+                        COPY,
+                        scale=1.0 / DYNAMIC,
+                        accum_out=emb[:, summary],
+                    )
 
-                if b == BLOCKS - 1:
-                    nc.sync.dma_start(out[channels, tokens], emb[:, tokens])
-                elif r == RECORDS - 1:
-                    nc.sync.dma_start(out[channels, :], emb[:])
+                    if b == BLOCKS - 1:
+                        nc.sync.dma_start(out[channels, start : start + TOKENS], emb[:, start : start + TOKENS])
+                    elif r == RECORDS - 1:
+                        nc.sync.dma_start(out[channels, :], emb[:])
+                else:
+                    tail = slice(start + HEAD, start + TOKENS)
+                    picked = tables[b][:].indirect(
+                        offsets[:, (start + HEAD) // 16 : (start + TOKENS) // 16]
+                    )
+                    nc.vector.tensor_tensor(emb[:, tail], picked, terms[:, HEAD:], ADD)
+                    nc.sync.dma_start(out[channels, tail], emb[:, tail])
+                    picked = tables[b][:].indirect(offsets[:, start // 16 : (start + HEAD) // 16])
+                    nc.vector.tensor_tensor(emb[:, start : start + HEAD], picked, terms[:, :HEAD], ADD)
+
+                    share = held.tile([P, 1], F32, name="share")
+                    scaled = scratch.tile([P, DYNAMIC], F32, name="scaled")
+                    nc.scalar.activation(
+                        scaled[:, : TOKENS - HEAD],
+                        emb[:, tail],
+                        COPY,
+                        scale=1.0 / (DYNAMIC * (HEAD - STATIC)),
+                        accum_out=share[:],
+                    )
+                    scaled = scratch.tile([P, DYNAMIC], F32, name="scaled")
+                    nc.scalar.activation(
+                        scaled[:, : HEAD - STATIC],
+                        emb[:, start + STATIC : start + HEAD],
+                        IDENTITY,
+                        bias=share[:],
+                        scale=1.0 / DYNAMIC,
+                        accum_out=emb[:, summary],
+                    )
+                    nc.sync.dma_start(out[channels, start : start + HEAD], emb[:, start : start + HEAD])

@@ -5,7 +5,6 @@ U16 = mybir.dt.uint16
 ADD = mybir.AluOpType.add
 MULT = mybir.AluOpType.mult
 COPY = mybir.ActivationFunctionType.Copy
-IDENTITY = mybir.ActivationFunctionType.Identity
 
 P = 128
 CHANNELS, CODES = 512, 4096
@@ -124,19 +123,16 @@ def tile_hybridsummaryencoder_kernel(
                     share = held.tile([P, 1], F32, name="share")
                     scaled = scratch.tile([P, DYNAMIC], F32, name="scaled")
                     nc.scalar.activation(
-                        scaled[:, : TOKENS - HEAD],
-                        emb[:, tail],
-                        COPY,
-                        scale=1.0 / (DYNAMIC * (HEAD - STATIC)),
-                        accum_out=share[:],
+                        scaled[:, : TOKENS - HEAD], emb[:, tail], COPY, scale=1.0 / DYNAMIC, accum_out=share[:]
                     )
                     scaled = scratch.tile([P, DYNAMIC], F32, name="scaled")
-                    nc.scalar.activation(
+                    nc.vector.tensor_scalar(
                         scaled[:, : HEAD - STATIC],
                         emb[:, start + STATIC : start + HEAD],
-                        IDENTITY,
-                        bias=share[:],
-                        scale=1.0 / DYNAMIC,
+                        1.0 / DYNAMIC,
+                        share[:],
+                        MULT,
+                        ADD,
                         accum_out=emb[:, summary],
                     )
                     nc.sync.dma_start(out[channels, start : start + HEAD], emb[:, start : start + HEAD])

@@ -17,11 +17,11 @@ PIECES = BLOCKS * RECORDS
 AHEAD = 4
 HEAD = 128
 
-ROW_VALUE = 0
-ROW_DYN = 1
-ROW_HAS = 126
-ROW_DAYS = 127
-FILLED = 126
+ROW_DYN = 94
+ROW_DAYS = 95
+ROW_VALUE = 96
+ROW_HAS = 97
+ROWS = 98
 
 FLOPS = 2 * 4 * CHANNELS * N
 
@@ -41,31 +41,30 @@ def tile_hybridsummaryencoder_kernel(
         offsets = held.tile([P, N // 16], U16, name="offsets")
         coefs = held.tile([P, CHANNELS], F32, name="coefs")
         features = held.tile([P, N], F32, name="features")
-        value_row = held.tile([1, N], F32, name="value_row")
-        has_row = held.tile([1, N], F32, name="has_row")
+        values = held.tile([P, N], F32, name="values")
         by_record = features[:].rearrange("k (r t) -> k r t", t=TOKENS)
 
-        nc.vector.memset(by_record[:, :, :STATIC], 0.0)
-        nc.vector.memset(coefs[:FILLED, :], 0.0)
-        nc.vector.memset(by_record[:FILLED, :, STATIC:], 1.0)
+        nc.vector.memset(by_record[: ROW_DAYS + 1, :, :STATIC], 0.0)
+        nc.vector.memset(coefs[:ROW_DYN, :], 0.0)
+        nc.vector.memset(by_record[:ROW_DAYS, :, STATIC:], 1.0)
 
-        nc.sync.dma_start(value_row[:], value)
-        nc.sync.dma_start(has_row[:], has_value)
+        nc.sync.dma_start(values[ROW_VALUE : ROW_VALUE + 1, :], value)
+        nc.sync.dma_start(features[ROW_VALUE : ROW_HAS + 1, :], has_value.to_broadcast([2, N]))
         nc.sync.dma_start(
             by_record[ROW_DAYS : ROW_DAYS + 1, :, STATIC:],
             days.rearrange("o (r t) -> o r t", t=TOKENS)[:, :, STATIC:],
         )
-        for row, vector in ((ROW_HAS, val_b), (ROW_DAYS, date_w), (ROW_VALUE, val_w), (ROW_DYN, date_b)):
+        for row, vector in ((ROW_VALUE, val_w), (ROW_HAS, val_b), (ROW_DAYS, date_w), (ROW_DYN, date_b)):
             nc.sync.dma_start(coefs[row : row + 1, :], vector.rearrange("c o -> o c"))
-        nc.sync.dma_start(features[ROW_HAS : ROW_HAS + 1, :], has_value)
+        nc.sync.dma_start(tables[0][:], table[:P, :])
         nc.sync.dma_start(offsets[:], offs)
-        for b in range(BLOCKS):
+        for b in range(1, BLOCKS):
             nc.sync.dma_start(tables[b][:], table[b * P : (b + 1) * P, :])
 
         for r in range(RECORDS):
-            tokens = slice(r * TOKENS, (r + 1) * TOKENS)
+            product_row = features[ROW_VALUE : ROW_VALUE + 1, r * TOKENS : (r + 1) * TOKENS]
             nc.vector.tensor_tensor(
-                features[ROW_VALUE : ROW_VALUE + 1, tokens], value_row[:, tokens], has_row[:, tokens], MULT
+                product_row, values[ROW_VALUE : ROW_VALUE + 1, r * TOKENS : (r + 1) * TOKENS], product_row, MULT
             )
 
         terms_of = {}
@@ -76,8 +75,8 @@ def tile_hybridsummaryencoder_kernel(
                 product = psum.tile([P, TOKENS], F32, name="product")
                 nc.tensor.matmul(
                     product[:],
-                    coefs[:, b * P : (b + 1) * P],
-                    features[:, r * TOKENS : (r + 1) * TOKENS],
+                    coefs[:ROWS, b * P : (b + 1) * P],
+                    features[:ROWS, r * TOKENS : (r + 1) * TOKENS],
                     start=True,
                     stop=True,
                 )

@@ -16,6 +16,7 @@ LIST_COLUMNS = TOKENS // 16
 PIECES = BLOCKS * RECORDS
 AHEAD = 4
 HEAD = 128
+RECORDS_A_STORE = (4, 4, 2, 1)
 
 ROW_DYN = 94
 ROW_DAYS = 95
@@ -105,10 +106,9 @@ def tile_hybridsummaryencoder_kernel(
                         accum_out=emb[:, summary],
                     )
 
-                    if b == BLOCKS - 1:
-                        nc.sync.dma_start(out[channels, start : start + TOKENS], emb[:, start : start + TOKENS])
-                    elif r == RECORDS - 1:
-                        nc.sync.dma_start(out[channels, :], emb[:])
+                    if (r + 1) % RECORDS_A_STORE[b] == 0:
+                        finished = slice((r + 1 - RECORDS_A_STORE[b]) * TOKENS, (r + 1) * TOKENS)
+                        nc.sync.dma_start(out[channels, finished], emb[:, finished])
                 else:
                     tail = slice(start + HEAD, start + TOKENS)
                     picked = tables[b][:].indirect(

import concourse.mybir as mybir

F32 = mybir.dt.float32
U16 = mybir.dt.uint16
ADD = mybir.AluOpType.add
MULT = mybir.AluOpType.mult
COPY = mybir.ActivationFunctionType.Copy

P = 128
CHANNELS, CODES = 512, 4096
RECORDS, TOKENS, STATIC = 4, 512, 32
DYNAMIC = TOKENS - STATIC
N = RECORDS * TOKENS
BLOCKS = CHANNELS // P
LIST_COLUMNS = TOKENS // 16
PIECES = BLOCKS * RECORDS
AHEAD = 4
HEAD = 128
RECORDS_A_STORE = (4, 4, 2, 1)

ROW_DYN = 94
ROW_DAYS = 95
ROW_VALUE = 96
ROW_HAS = 97
ROWS = 98

FLOPS = 2 * 4 * CHANNELS * N


def tile_hybridsummaryencoder_kernel(
    tc, table, days, value, has_value, date_w, date_b, val_w, val_b, offs, out
):
    nc = tc.nc
    with (
        tc.tile_pool(name="held", bufs=1) as held,
        tc.tile_pool(name="ahead", bufs=AHEAD + 2) as ahead,
        tc.tile_pool(name="scratch", bufs=2) as scratch,
        tc.psum_pool(name="psum", bufs=4) as psum,
    ):
        tables = [held.tile([P, CODES], F32, name=f"table{b}") for b in range(BLOCKS)]
        embs = [held.tile([P, N], F32, name=f"emb{b}") for b in range(BLOCKS)]
        offsets = held.tile([P, N // 16], U16, name="offsets")
        coefs = held.tile([P, CHANNELS], F32, name="coefs")
        features = held.tile([P, N], F32, name="features")
        values = held.tile([P, N], F32, name="values")
        by_record = features[:].rearrange("k (r t) -> k r t", t=TOKENS)

        nc.vector.memset(by_record[: ROW_DAYS + 1, :, :STATIC], 0.0)
        nc.vector.memset(coefs[:ROW_DYN, :], 0.0)
        nc.vector.memset(by_record[:ROW_DAYS, :, STATIC:], 1.0)

        nc.sync.dma_start(values[ROW_VALUE : ROW_VALUE + 1, :], value)
        nc.sync.dma_start(features[ROW_VALUE : ROW_HAS + 1, :], has_value.to_broadcast([2, N]))
        nc.sync.dma_start(
            by_record[ROW_DAYS : ROW_DAYS + 1, :, STATIC:],
            days.rearrange("o (r t) -> o r t", t=TOKENS)[:, :, STATIC:],
        )
        for row, vector in ((ROW_VALUE, val_w), (ROW_HAS, val_b), (ROW_DAYS, date_w), (ROW_DYN, date_b)):
            nc.sync.dma_start(coefs[row : row + 1, :], vector.rearrange("c o -> o c"))
        nc.sync.dma_start(tables[0][:], table[:P, :])
        nc.sync.dma_start(offsets[:], offs)
        for b in range(1, BLOCKS):
            nc.sync.dma_start(tables[b][:], table[b * P : (b + 1) * P, :])

        for r in range(RECORDS):
            product_row = features[ROW_VALUE : ROW_VALUE + 1, r * TOKENS : (r + 1) * TOKENS]
            nc.vector.tensor_tensor(
                product_row, values[ROW_VALUE : ROW_VALUE + 1, r * TOKENS : (r + 1) * TOKENS], product_row, MULT
            )

        terms_of = {}

        for step in range(PIECES + AHEAD):
            if step < PIECES:
                b, r = divmod(step, RECORDS)
                product = psum.tile([P, TOKENS], F32, name="product")
                nc.tensor.matmul(
                    product[:],
                    coefs[:ROWS, b * P : (b + 1) * P],
                    features[:ROWS, r * TOKENS : (r + 1) * TOKENS],
                    start=True,
                    stop=True,
                )
                terms = ahead.tile([P, TOKENS], F32, name="terms")
                nc.scalar.copy(terms[:], product[:])
                terms_of[step] = terms

            if step >= AHEAD:
                b, r = divmod(step - AHEAD, RECORDS)
                emb = embs[b]
                terms = terms_of[step - AHEAD]
                channels = slice(b * P, (b + 1) * P)
                start = r * TOKENS
                summary = slice(start + STATIC, start + STATIC + 1)

                if step - AHEAD < PIECES - 1:
                    picked = tables[b][:].indirect(offsets[:, r * LIST_COLUMNS : (r + 1) * LIST_COLUMNS])
                    nc.vector.tensor_tensor(emb[:, start : start + TOKENS], picked, terms[:], ADD)

                    scaled = scratch.tile([P, DYNAMIC], F32, name="scaled")
                    nc.scalar.activation(
                        scaled[:],
                        emb[:, start + STATIC : start + TOKENS],
                        COPY,
                        scale=1.0 / DYNAMIC,
                        accum_out=emb[:, summary],
                    )

                    if (r + 1) % RECORDS_A_STORE[b] == 0:
                        finished = slice((r + 1 - RECORDS_A_STORE[b]) * TOKENS, (r + 1) * TOKENS)
                        nc.sync.dma_start(out[channels, finished], emb[:, finished])
                else:
                    tail = slice(start + HEAD, start + TOKENS)
                    picked = tables[b][:].indirect(
                        offsets[:, (start + HEAD) // 16 : (start + TOKENS) // 16]
                    )
                    nc.vector.tensor_tensor(emb[:, tail], picked, terms[:, HEAD:], ADD)
                    nc.sync.dma_start(out[channels, tail], emb[:, tail])
                    picked = tables[b][:].indirect(offsets[:, start // 16 : (start + HEAD) // 16])
                    nc.vector.tensor_tensor(emb[:, start : start + HEAD], picked, terms[:, :HEAD], ADD)

                    share = held.tile([P, 1], F32, name="share")
                    scaled = scratch.tile([P, DYNAMIC], F32, name="scaled")
                    nc.scalar.activation(
                        scaled[:, : TOKENS - HEAD], emb[:, tail], COPY, scale=1.0 / DYNAMIC, accum_out=share[:]
                    )
                    scaled = scratch.tile([P, DYNAMIC], F32, name="scaled")
                    nc.vector.tensor_scalar(
                        scaled[:, : HEAD - STATIC],
                        emb[:, start + STATIC : start + HEAD],
                        1.0 / DYNAMIC,
                        share[:],
                        MULT,
                        ADD,
                        accum_out=emb[:, summary],
                    )
                    nc.sync.dma_start(out[channels, start : start + HEAD], emb[:, start : start + HEAD])
